import numpy as np
import ml_dtypes


def mxq(x, axis, fmt="e4m3"):
    dtype, down = {"e4m3": (ml_dtypes.float8_e4m3fn, 7), "e5m2": (ml_dtypes.float8_e5m2, 14)}[fmt]
    v = np.moveaxis(np.asarray(x, np.float32).astype(ml_dtypes.bfloat16).astype(np.float64), axis, -1)
    blocks = v.reshape(v.shape[:-1] + (-1, 32))
    amax = np.abs(blocks).max(-1, keepdims=True)
    byte = np.maximum(np.where(amax > 0, np.frexp(amax)[1] - 1 + 127, 0) - down, 1)
    scale = np.exp2(byte - 127.0)
    codes = (blocks / scale).astype(np.float32).astype(dtype).astype(np.float64)
    return np.moveaxis((codes * scale).reshape(v.shape), -1, axis)


WIDE = False


def mx_kscale(k):
    if not WIDE:
        return np.ones(k)
    levels = np.array([10, -10, 5, -5, 0])
    if k % 512:
        return np.exp2(np.random.permutation(np.resize(levels, k // 32))).repeat(32)
    a = np.empty((k // 512, 16))
    for p in range(k // 512):
        a[p, :8] = np.random.permutation(np.resize(levels, 8))
        for g in range(8):
            far = levels[np.abs(levels - a[p, g]) >= 10]
            a[p, g + 8] = far[np.random.randint(len(far))]
    return np.exp2(a.ravel()).repeat(32)


BF16 = ml_dtypes.bfloat16


def bf(x):
    return np.asarray(x, np.float32).astype(BF16)


def f64(x):
    return np.asarray(x).astype(np.float64)


N, F, K, D, E = 128, 512, 512, 512, 512
SIG = 2.0
PS = 16.0


def setup_inputs():
    t, sx = mx_kscale(K), mx_kscale(F)
    s = np.concatenate([sx, np.ones(E)])
    g = SIG * np.random.standard_normal((N, K))
    e = np.exp(g - g.max(-1, keepdims=True))
    w = e / e.sum(-1, keepdims=True) * (np.random.uniform(size=K) * PS)[None, :]
    return {"att_prior": bf(w * t[None, :]),
            "dic": bf(np.random.standard_normal((K, D)) / t[:, None]),
            "x": bf(np.random.standard_normal((N, F)) * sx[None, :]),
            "cs_w": bf(np.random.standard_normal((K, F + E)) * (F + E) ** -0.5 / s[None, :]),
            "cs_b": bf(np.random.standard_normal(K) * 0.1)}


def reference(att_prior, dic, x, cs_w, cs_b):
    z = mxq(f64(att_prior), 1, "e4m3") @ mxq(f64(dic), 0, "e4m3")
    xz = np.concatenate([f64(x), z], axis=1)
    causal_logits = (mxq(xz, 1, "e4m3") @ mxq(f64(cs_w), 1, "e4m3").T) + f64(cs_b)
    return causal_logits, z

@@ -1,0 +1,186 @@
+from contextlib import ExitStack
+
+import concourse.mybir as mybir
+from concourse.masks import make_identity
+
+BF16 = mybir.dt.bfloat16
+F32 = mybir.dt.float32
+U32 = mybir.dt.uint32
+U8 = mybir.dt.uint8
+FP8X4 = mybir.dt.float8_e4m3fn_x4
+
+P = 128
+PACK = 4
+K_PASS = P * PACK
+D = 512
+OUT = 512
+W_PASSES = 2
+GROUPS = D // P
+OUT_CHUNKS = OUT // P
+CHUNKS_PER_BANK = 2
+VECTOR_GROUPS = 3
+
+FLOPS = 2 * P * K_PASS * D + 2 * P * (W_PASSES * K_PASS) * OUT
+
+
+def tile_visualdeconfounder_pb_s_kernel(tc, att_prior, dic, x, cs_w, cs_b, out_0, out_1):
+    nc = tc.nc
+    with ExitStack() as ctx:
+        keep = ctx.enter_context(tc.tile_pool(name="keep", bufs=1))
+        turned = ctx.enter_context(tc.psum_pool(name="turned", bufs=3))
+        sums = ctx.enter_context(tc.psum_pool(name="sums", bufs=1))
+        finished = ctx.enter_context(tc.psum_pool(name="finished", bufs=2))
+        ctx.enter_context(tc.manual_schedule())
+
+        ident = keep.tile([P, P], F32)
+        make_identity(nc, ident[:])
+        bias_rows = keep.tile([P, OUT], BF16)
+        nc.vector.memset(bias_rows[:], 0.0)
+        ones = keep.tile([P, P], BF16)
+        nc.vector.memset(ones[:], 1.0)
+
+        dic_raw = keep.tile([P, PACK, D], BF16)
+        nc.sync.dma_start(out=dic_raw[:], in_=dic.rearrange("(p t) c -> p t c", t=PACK))
+        nc.sync.dma_start(out=bias_rows[0:1, :], in_=cs_b.unsqueeze(0))
+        att_sb = keep.tile([P, K_PASS], BF16)
+        nc.sync.dma_start(out=att_sb[:], in_=att_prior)
+        x_sb = keep.tile([P, K_PASS], BF16)
+        nc.sync.dma_start(out=x_sb[:], in_=x)
+        w_sb = keep.tile([P, OUT_CHUNKS, W_PASSES * K_PASS], BF16)
+        for oc in range(OUT_CHUNKS):
+            nc.sync.dma_start(out=w_sb[:, oc, :], in_=cs_w[oc * P : (oc + 1) * P, :])
+
+        def turn(rows_sb, grouped):
+            passes = grouped.shape[1]
+            words = rows_sb.bitcast(F32)
+            words_t = turned.tile([P, passes * 2, P], F32, tag="turned")
+            for gu in range(passes * 2):
+                first = 2 * P * (gu // 2) + gu % 2
+                nc.tensor.transpose(words_t[:, gu, :], words[:, first : first + 2 * P - 1 : 2], ident[:])
+            nc.scalar.copy(out=grouped.bitcast(F32), in_=words_t[:].rearrange("p (g u) r -> p g r u", g=passes))
+
+        def quantise(grouped, codes, scales):
+            nc.vector.quantize_mx(
+                out=codes.bitcast(FP8X4), scales=scales, in_=grouped.rearrange("p c t -> p (c t)")
+            )
+
+        bias_ps = sums.tile([P, OUT], BF16)
+        nc.tensor.matmul(out=bias_ps[:], lhsT=ones[:], rhs=bias_rows[:], start=True, stop=True)
+
+        dic_grouped = keep.tile([P, D, PACK], BF16, align_bytes=64)
+        dic_sorted = dic_raw[:].rearrange("p t (q j) -> p j q t", j=GROUPS)
+        for j in range(GROUPS):
+            engine_copy = nc.vector.tensor_copy if j < VECTOR_GROUPS else nc.scalar.copy
+            engine_copy(out=dic_grouped[:, j * P : (j + 1) * P, :], in_=dic_sorted[:, j])
+
+        att_grouped = keep.tile([P, 1, P, PACK], BF16, align_bytes=64)
+        turn(att_sb[:], att_grouped[:])
+        x_grouped = keep.tile([P, 1, P, PACK], BF16, align_bytes=64)
+        turn(x_sb[:], x_grouped[:])
+
+        dic_codes = keep.tile([P, D], U32, align_bytes=64)
+        dic_scales = keep.tile([P, D], U8, align_bytes=64)
+        for j in range(GROUPS):
+            cols = slice(j * P, (j + 1) * P)
+            quantise(dic_grouped[:, cols, :], dic_codes[:, cols], dic_scales[:, cols])
+        att_codes = keep.tile([P, P], U32, align_bytes=64)
+        att_scales = keep.tile([P, P], U8, align_bytes=64)
+        quantise(att_grouped[:, 0], att_codes[:], att_scales[:])
+
+        w_grouped = keep.tile([P, OUT_CHUNKS, W_PASSES, P, PACK], BF16, align_bytes=64)
+        w_codes = keep.tile([P, OUT_CHUNKS, W_PASSES, P], U32, align_bytes=64)
+        w_scales = keep.tile([P, OUT_CHUNKS, W_PASSES, P], U8, align_bytes=64)
+
+        def turn_w(oc):
+            turn(w_sb[:, oc, :], w_grouped[:, oc])
+
+        def quantise_w(oc):
+            quantise(
+                w_grouped[:, oc].rearrange("p g o t -> p (g o) t"),
+                w_codes[:, oc].rearrange("p g o -> p (g o)"),
+                w_scales[:, oc].rearrange("p g o -> p (g o)"),
+            )
+
+        turn_w(0)
+        turn_w(1)
+
+        zt_ps = sums.tile([P, GROUPS, P], F32)
+        for j in range(GROUPS):
+            cols = slice(j * P, (j + 1) * P)
+            nc.tensor.matmul_mx(
+                out=zt_ps[:, j, :],
+                lhsT=dic_codes[:, cols].bitcast(FP8X4),
+                lhsT_scale=dic_scales[:, cols],
+                rhs=att_codes[:].bitcast(FP8X4),
+                rhs_scale=att_scales[:],
+                start=True,
+                stop=True,
+            )
+
+        x_codes = keep.tile([P, P], U32, align_bytes=64)
+        x_scales = keep.tile([P, P], U8, align_bytes=64)
+        quantise(x_grouped[:, 0], x_codes[:], x_scales[:])
+        bias_sb = keep.tile([P, OUT], BF16)
+        nc.vector.tensor_copy(out=bias_sb[:], in_=bias_ps[:])
+        z_grouped = keep.tile([P, P, PACK], BF16, align_bytes=64)
+        nc.vector.tensor_copy(out=z_grouped[:], in_=zt_ps[:].rearrange("q j n -> q n j"))
+        quantise_w(0)
+        z_codes = keep.tile([P, P], U32, align_bytes=64)
+        z_scales = keep.tile([P, P], U8, align_bytes=64)
+        quantise(z_grouped[:], z_codes[:], z_scales[:])
+        quantise_w(1)
+
+        turn_w(2)
+        turn_w(3)
+
+        quantise_w(2)
+        quantise_w(3)
+
+        z_ps = sums.tile([P, D], F32)
+        nc.tensor.matmul_mx(
+            out=z_ps[:],
+            lhsT=att_codes[:].bitcast(FP8X4),
+            lhsT_scale=att_scales[:],
+            rhs=dic_codes[:].bitcast(FP8X4),
+            rhs_scale=dic_scales[:],
+            start=True,
+            stop=True,
+        )
+        z_sb = keep.tile([P, D], F32)
+        nc.scalar.copy(
+            out=z_sb[:].rearrange("n (q j) -> n q j", j=GROUPS),
+            in_=z_ps[:].rearrange("n (j q) -> n q j", j=GROUPS),
+        )
+        nc.sync.dma_start(out=out_1, in_=z_sb[:])
+
+        logits_sb = keep.tile([P, OUT], F32)
+        for h in range(OUT_CHUNKS // CHUNKS_PER_BANK):
+            logits_ps = finished.tile([P, CHUNKS_PER_BANK, P], F32)
+            for c in range(CHUNKS_PER_BANK):
+                oc = h * CHUNKS_PER_BANK + c
+                nc.tensor.matmul_mx(
+                    out=logits_ps[:, c, :],
+                    lhsT=x_codes[:].bitcast(FP8X4),
+                    lhsT_scale=x_scales[:],
+                    rhs=w_codes[:, oc, 0, :].bitcast(FP8X4),
+                    rhs_scale=w_scales[:, oc, 0, :],
+                    start=True,
+                    stop=False,
+                )
+                nc.tensor.matmul_mx(
+                    out=logits_ps[:, c, :],
+                    lhsT=z_codes[:].bitcast(FP8X4),
+                    lhsT_scale=z_scales[:],
+                    rhs=w_codes[:, oc, 1, :].bitcast(FP8X4),
+                    rhs_scale=w_scales[:, oc, 1, :],
+                    start=False,
+                    stop=True,
+                )
+            cols = slice(h * CHUNKS_PER_BANK * P, (h + 1) * CHUNKS_PER_BANK * P)
+            nc.vector.tensor_tensor(
+                out=logits_sb[:, cols],
+                in0=logits_ps[:].rearrange("n c o -> n (c o)"),
+                in1=bias_sb[:, cols],
+                op=mybir.AluOpType.add,
+            )
+            nc.sync.dma_start(out=out_0[:, cols], in_=logits_sb[:, cols])

@@ -16,6 +16,8 @@ D = 512
 OUT = 512
 W_PASSES = 2
 GROUPS = D // P
+WARM_COLS = 256
+WARM_PASSES = 8
 OUT_CHUNKS = OUT // P
 CHUNKS_PER_BANK = 2
 VECTOR_GROUPS = 3
@@ -34,8 +36,10 @@ def tile_visualdeconfounder_pb_s_kernel(tc, att_prior, dic, x, cs_w, cs_b, out_0
 
         ident = keep.tile([P, P], F32)
         make_identity(nc, ident[:])
+        zeros = keep.tile([P, WARM_COLS, PACK], BF16, align_bytes=64)
+        nc.vector.memset(zeros[:].rearrange("p c t -> p (c t)").bitcast(U32), 0)
         bias_rows = keep.tile([P, OUT], BF16)
-        nc.vector.memset(bias_rows[:], 0.0)
+        nc.vector.memset(bias_rows[:].bitcast(U32), 0)
         ones = keep.tile([P, P], BF16)
         nc.vector.memset(ones[:], 1.0)
 
@@ -62,6 +66,21 @@ def tile_visualdeconfounder_pb_s_kernel(tc, att_prior, dic, x, cs_w, cs_b, out_0
         def quantise(grouped, codes, scales):
             nc.vector.quantize_mx(
                 out=codes.bitcast(FP8X4), scales=scales, in_=grouped.rearrange("p c t -> p (c t)")
+            )
+
+        zero_codes = keep.tile([P, WARM_COLS], U32, align_bytes=64)
+        zero_scales = keep.tile([P, WARM_COLS], U8, align_bytes=64)
+        quantise(zeros[:], zero_codes[:], zero_scales[:])
+        z_ps = sums.tile([P, D], F32)
+        for i in range(WARM_PASSES):
+            nc.tensor.matmul_mx(
+                out=z_ps[:, :WARM_COLS],
+                lhsT=zero_codes[:, :P].bitcast(FP8X4),
+                lhsT_scale=zero_scales[:, :P],
+                rhs=zero_codes[:].bitcast(FP8X4),
+                rhs_scale=zero_scales[:],
+                start=True,
+                stop=True,
             )
 
         bias_ps = sums.tile([P, OUT], BF16)
@@ -117,6 +136,15 @@ def tile_visualdeconfounder_pb_s_kernel(tc, att_prior, dic, x, cs_w, cs_b, out_0
                 stop=True,
             )
 
+        nc.tensor.matmul_mx(
+            out=z_ps[:],
+            lhsT=att_codes[:].bitcast(FP8X4),
+            lhsT_scale=att_scales[:],
+            rhs=dic_codes[:].bitcast(FP8X4),
+            rhs_scale=dic_scales[:],
+            start=True,
+            stop=True,
+        )
         x_codes = keep.tile([P, P], U32, align_bytes=64)
         x_scales = keep.tile([P, P], U8, align_bytes=64)
         quantise(x_grouped[:, 0], x_codes[:], x_scales[:])
@@ -136,16 +164,6 @@ def tile_visualdeconfounder_pb_s_kernel(tc, att_prior, dic, x, cs_w, cs_b, out_0
         quantise_w(2)
         quantise_w(3)
 
-        z_ps = sums.tile([P, D], F32)
-        nc.tensor.matmul_mx(
-            out=z_ps[:],
-            lhsT=att_codes[:].bitcast(FP8X4),
-            lhsT_scale=att_scales[:],
-            rhs=dic_codes[:].bitcast(FP8X4),
-            rhs_scale=dic_scales[:],
-            start=True,
-            stop=True,
-        )
         z_sb = keep.tile([P, D], F32)
         nc.scalar.copy(
             out=z_sb[:].rearrange("n (q j) -> n q j", j=GROUPS),

@@ -20,7 +20,7 @@ WARM_COLS = 256
 WARM_PASSES = 8
 OUT_CHUNKS = OUT // P
 CHUNKS_PER_BANK = 2
-VECTOR_GROUPS = 3
+VECTOR_Q = 80
 
 FLOPS = 2 * P * K_PASS * D + 2 * P * (W_PASSES * K_PASS) * OUT
 
@@ -87,10 +87,10 @@ def tile_visualdeconfounder_pb_s_kernel(tc, att_prior, dic, x, cs_w, cs_b, out_0
         nc.tensor.matmul(out=bias_ps[:], lhsT=ones[:], rhs=bias_rows[:], start=True, stop=True)
 
         dic_grouped = keep.tile([P, D, PACK], BF16, align_bytes=64)
-        dic_sorted = dic_raw[:].rearrange("p t (q j) -> p j q t", j=GROUPS)
-        for j in range(GROUPS):
-            engine_copy = nc.vector.tensor_copy if j < VECTOR_GROUPS else nc.scalar.copy
-            engine_copy(out=dic_grouped[:, j * P : (j + 1) * P, :], in_=dic_sorted[:, j])
+        dic_read = dic_raw[:].rearrange("p t (q j) -> p q j t", j=GROUPS)
+        dic_write = dic_grouped[:].rearrange("p (j q) t -> p q j t", j=GROUPS)
+        nc.vector.tensor_copy(out=dic_write[:, :VECTOR_Q], in_=dic_read[:, :VECTOR_Q])
+        nc.scalar.copy(out=dic_write[:, VECTOR_Q:], in_=dic_read[:, VECTOR_Q:])
 
         att_grouped = keep.tile([P, 1, P, PACK], BF16, align_bytes=64)
         turn(att_sb[:], att_grouped[:])

@@ -16,11 +16,12 @@ D = 512
 OUT = 512
 W_PASSES = 2
 GROUPS = D // P
+OUT_CHUNKS = OUT // P
+LAST = OUT_CHUNKS - 1
 WARM_COLS = 256
 WARM_PASSES = 8
-OUT_CHUNKS = OUT // P
-CHUNKS_PER_BANK = 2
-VECTOR_Q = 80
+
+VECTOR_Q = 88
 
 FLOPS = 2 * P * K_PASS * D + 2 * P * (W_PASSES * K_PASS) * OUT
 
@@ -29,22 +30,14 @@ def tile_visualdeconfounder_pb_s_kernel(tc, att_prior, dic, x, cs_w, cs_b, out_0
     nc = tc.nc
     with ExitStack() as ctx:
         keep = ctx.enter_context(tc.tile_pool(name="keep", bufs=1))
-        turned = ctx.enter_context(tc.psum_pool(name="turned", bufs=3))
+        turned = ctx.enter_context(tc.psum_pool(name="turned", bufs=4))
         sums = ctx.enter_context(tc.psum_pool(name="sums", bufs=1))
-        finished = ctx.enter_context(tc.psum_pool(name="finished", bufs=2))
         ctx.enter_context(tc.manual_schedule())
-
-        ident = keep.tile([P, P], F32)
-        make_identity(nc, ident[:])
-        zeros = keep.tile([P, WARM_COLS, PACK], BF16, align_bytes=64)
-        nc.vector.memset(zeros[:].rearrange("p c t -> p (c t)").bitcast(U32), 0)
-        bias_rows = keep.tile([P, OUT], BF16)
-        nc.vector.memset(bias_rows[:].bitcast(U32), 0)
-        ones = keep.tile([P, P], BF16)
-        nc.vector.memset(ones[:], 1.0)
 
         dic_raw = keep.tile([P, PACK, D], BF16)
         nc.sync.dma_start(out=dic_raw[:], in_=dic.rearrange("(p t) c -> p t c", t=PACK))
+        bias_rows = keep.tile([P, OUT], BF16)
+        nc.vector.memset(bias_rows[:].bitcast(U32), 0)
         nc.sync.dma_start(out=bias_rows[0:1, :], in_=cs_b.unsqueeze(0))
         att_sb = keep.tile([P, K_PASS], BF16)
         nc.sync.dma_start(out=att_sb[:], in_=att_prior)
@@ -54,27 +47,83 @@ def tile_visualdeconfounder_pb_s_kernel(tc, att_prior, dic, x, cs_w, cs_b, out_0
         for oc in range(OUT_CHUNKS):
             nc.sync.dma_start(out=w_sb[:, oc, :], in_=cs_w[oc * P : (oc + 1) * P, :])
 
-        def turn(rows_sb, grouped):
-            passes = grouped.shape[1]
+        ident = keep.tile([P, P], F32)
+        make_identity(nc, ident[:])
+        zeros = keep.tile([P, WARM_COLS, PACK], BF16, align_bytes=64)
+        nc.vector.memset(zeros[:].rearrange("p c t -> p (c t)").bitcast(U32), 0)
+        ones = keep.tile([P, P], BF16)
+        nc.vector.memset(ones[:], 1.0)
+
+        def turn(rows_sb):
             words = rows_sb.bitcast(F32)
-            words_t = turned.tile([P, passes * 2, P], F32, tag="turned")
-            for gu in range(passes * 2):
+            tiles = words.shape[1] // P
+            words_t = turned.tile([P, PACK, P], F32, tag="turned")
+            for gu in range(tiles):
                 first = 2 * P * (gu // 2) + gu % 2
                 nc.tensor.transpose(words_t[:, gu, :], words[:, first : first + 2 * P - 1 : 2], ident[:])
-            nc.scalar.copy(out=grouped.bitcast(F32), in_=words_t[:].rearrange("p (g u) r -> p g r u", g=passes))
+            return words_t[:, :tiles, :]
+
+        def regroup(engine_copy, words_t, grouped):
+            engine_copy(out=grouped.bitcast(F32), in_=words_t.rearrange("p (g u) r -> p g r u", u=2))
 
         def quantise(grouped, codes, scales):
             nc.vector.quantize_mx(
                 out=codes.bitcast(FP8X4), scales=scales, in_=grouped.rearrange("p c t -> p (c t)")
             )
 
+        scalar_copy = nc.scalar.copy
+        vector_copy = nc.vector.tensor_copy
+
+        att_grouped = keep.tile([P, 1, P, PACK], BF16, align_bytes=64)
+        att_codes = keep.tile([P, P], U32, align_bytes=64)
+        att_scales = keep.tile([P, P], U8, align_bytes=64)
+        x_grouped = keep.tile([P, 1, P, PACK], BF16, align_bytes=64)
+        x_codes = keep.tile([P, P], U32, align_bytes=64)
+        x_scales = keep.tile([P, P], U8, align_bytes=64)
+        dic_grouped = keep.tile([P, D, PACK], BF16, align_bytes=64)
+        dic_codes = keep.tile([P, D], U32, align_bytes=64)
+        dic_scales = keep.tile([P, D], U8, align_bytes=64)
+        w_grouped = keep.tile([P, OUT_CHUNKS, W_PASSES, P, PACK], BF16, align_bytes=64)
+        w_codes = keep.tile([P, OUT_CHUNKS, W_PASSES, P], U32, align_bytes=64)
+        w_scales = keep.tile([P, OUT_CHUNKS, W_PASSES, P], U8, align_bytes=64)
+        z_grouped = keep.tile([P, P, PACK], BF16, align_bytes=64)
+        z_codes = keep.tile([P, P], U32, align_bytes=64)
+        z_scales = keep.tile([P, P], U8, align_bytes=64)
+        bias_sb = keep.tile([P, OUT], BF16)
+        z_sb = keep.tile([P, D], F32)
+        logits_sb = keep.tile([P, OUT], F32)
+
+        def quantise_w(oc, first=0, last=W_PASSES):
+            quantise(
+                w_grouped[:, oc, first:last].rearrange("p g o t -> p (g o) t"),
+                w_codes[:, oc, first:last].rearrange("p g o -> p (g o)"),
+                w_scales[:, oc, first:last].rearrange("p g o -> p (g o)"),
+            )
+
+        def multiply(acc, oc, g):
+            codes, scales = ((x_codes, x_scales), (z_codes, z_scales))[g]
+            nc.tensor.matmul_mx(
+                out=acc,
+                lhsT=codes[:].bitcast(FP8X4),
+                lhsT_scale=scales[:],
+                rhs=w_codes[:, oc, g, :].bitcast(FP8X4),
+                rhs_scale=w_scales[:, oc, g, :],
+                start=g == 0,
+                stop=g == W_PASSES - 1,
+            )
+
+        def finish(acc, first, last):
+            cols = slice(first * P, last * P)
+            nc.vector.tensor_tensor(out=logits_sb[:, cols], in0=acc, in1=bias_sb[:, cols], op=mybir.AluOpType.add)
+            nc.sync.dma_start(out=out_0[:, cols], in_=logits_sb[:, cols])
+
         zero_codes = keep.tile([P, WARM_COLS], U32, align_bytes=64)
         zero_scales = keep.tile([P, WARM_COLS], U8, align_bytes=64)
         quantise(zeros[:], zero_codes[:], zero_scales[:])
-        z_ps = sums.tile([P, D], F32)
+        warm_ps = sums.tile([P, WARM_COLS], F32, tag="rows")
         for i in range(WARM_PASSES):
             nc.tensor.matmul_mx(
-                out=z_ps[:, :WARM_COLS],
+                out=warm_ps[:],
                 lhsT=zero_codes[:, :P].bitcast(FP8X4),
                 lhsT_scale=zero_scales[:, :P],
                 rhs=zero_codes[:].bitcast(FP8X4),
@@ -83,47 +132,26 @@ def tile_visualdeconfounder_pb_s_kernel(tc, att_prior, dic, x, cs_w, cs_b, out_0
                 stop=True,
             )
 
-        bias_ps = sums.tile([P, OUT], BF16)
-        nc.tensor.matmul(out=bias_ps[:], lhsT=ones[:], rhs=bias_rows[:], start=True, stop=True)
-
-        dic_grouped = keep.tile([P, D, PACK], BF16, align_bytes=64)
         dic_read = dic_raw[:].rearrange("p t (q j) -> p q j t", j=GROUPS)
         dic_write = dic_grouped[:].rearrange("p (j q) t -> p q j t", j=GROUPS)
-        nc.vector.tensor_copy(out=dic_write[:, :VECTOR_Q], in_=dic_read[:, :VECTOR_Q])
-        nc.scalar.copy(out=dic_write[:, VECTOR_Q:], in_=dic_read[:, VECTOR_Q:])
-
-        att_grouped = keep.tile([P, 1, P, PACK], BF16, align_bytes=64)
-        turn(att_sb[:], att_grouped[:])
-        x_grouped = keep.tile([P, 1, P, PACK], BF16, align_bytes=64)
-        turn(x_sb[:], x_grouped[:])
-
-        dic_codes = keep.tile([P, D], U32, align_bytes=64)
-        dic_scales = keep.tile([P, D], U8, align_bytes=64)
-        for j in range(GROUPS):
-            cols = slice(j * P, (j + 1) * P)
+        vector_copy(out=dic_write[:, :VECTOR_Q], in_=dic_read[:, :VECTOR_Q])
+        scalar_copy(out=dic_write[:, VECTOR_Q:], in_=dic_read[:, VECTOR_Q:])
+        att_t = turn(att_sb[:])
+        regroup(scalar_copy, att_t, att_grouped[:])
+        x_t = turn(x_sb[:])
+        regroup(scalar_copy, x_t, x_grouped[:])
+        bias_ps = sums.tile([P, OUT], BF16, tag="rows")
+        nc.tensor.matmul(out=bias_ps[:], lhsT=ones[:], rhs=bias_rows[:], start=True, stop=True)
+        for j in range(0, GROUPS, 2):
+            cols = slice(j * P, (j + 2) * P)
             quantise(dic_grouped[:, cols, :], dic_codes[:, cols], dic_scales[:, cols])
-        att_codes = keep.tile([P, P], U32, align_bytes=64)
-        att_scales = keep.tile([P, P], U8, align_bytes=64)
         quantise(att_grouped[:, 0], att_codes[:], att_scales[:])
+        quantise(x_grouped[:, 0], x_codes[:], x_scales[:])
+        vector_copy(out=bias_sb[:], in_=bias_ps[:])
 
-        w_grouped = keep.tile([P, OUT_CHUNKS, W_PASSES, P, PACK], BF16, align_bytes=64)
-        w_codes = keep.tile([P, OUT_CHUNKS, W_PASSES, P], U32, align_bytes=64)
-        w_scales = keep.tile([P, OUT_CHUNKS, W_PASSES, P], U8, align_bytes=64)
-
-        def turn_w(oc):
-            turn(w_sb[:, oc, :], w_grouped[:, oc])
-
-        def quantise_w(oc):
-            quantise(
-                w_grouped[:, oc].rearrange("p g o t -> p (g o) t"),
-                w_codes[:, oc].rearrange("p g o -> p (g o)"),
-                w_scales[:, oc].rearrange("p g o -> p (g o)"),
-            )
-
-        turn_w(0)
-        turn_w(1)
-
-        zt_ps = sums.tile([P, GROUPS, P], F32)
+        for oc in range(2):
+            regroup(scalar_copy, turn(w_sb[:, oc, :]), w_grouped[:, oc])
+        zt_ps = sums.tile([P, GROUPS, P], F32, tag="zt")
         for j in range(GROUPS):
             cols = slice(j * P, (j + 1) * P)
             nc.tensor.matmul_mx(
@@ -135,7 +163,19 @@ def tile_visualdeconfounder_pb_s_kernel(tc, att_prior, dic, x, cs_w, cs_b, out_0
                 start=True,
                 stop=True,
             )
+        scalar_copy(out=z_grouped[:], in_=zt_ps[:].rearrange("q j n -> q n j"))
+        quantise_w(0)
+        quantise_w(1)
+        regroup(vector_copy, turn(w_sb[:, 2, :K_PASS]), w_grouped[:, 2, 0:1])
+        regroup(scalar_copy, turn(w_sb[:, 2, K_PASS:]), w_grouped[:, 2, 1:2])
+        quantise(z_grouped[:], z_codes[:], z_scales[:])
+        regroup(scalar_copy, turn(w_sb[:, LAST, :K_PASS]), w_grouped[:, LAST, 0:1])
+        regroup(scalar_copy, turn(w_sb[:, LAST, K_PASS:]), w_grouped[:, LAST, 1:2])
+        quantise_w(2)
+        quantise_w(LAST, 0, 1)
+        quantise_w(LAST, 1, 2)
 
+        z_ps = sums.tile([P, D], F32, tag="rows")
         nc.tensor.matmul_mx(
             out=z_ps[:],
             lhsT=att_codes[:].bitcast(FP8X4),
@@ -145,60 +185,22 @@ def tile_visualdeconfounder_pb_s_kernel(tc, att_prior, dic, x, cs_w, cs_b, out_0
             start=True,
             stop=True,
         )
-        x_codes = keep.tile([P, P], U32, align_bytes=64)
-        x_scales = keep.tile([P, P], U8, align_bytes=64)
-        quantise(x_grouped[:, 0], x_codes[:], x_scales[:])
-        bias_sb = keep.tile([P, OUT], BF16)
-        nc.vector.tensor_copy(out=bias_sb[:], in_=bias_ps[:])
-        z_grouped = keep.tile([P, P, PACK], BF16, align_bytes=64)
-        nc.vector.tensor_copy(out=z_grouped[:], in_=zt_ps[:].rearrange("q j n -> q n j"))
-        quantise_w(0)
-        z_codes = keep.tile([P, P], U32, align_bytes=64)
-        z_scales = keep.tile([P, P], U8, align_bytes=64)
-        quantise(z_grouped[:], z_codes[:], z_scales[:])
-        quantise_w(1)
-
-        turn_w(2)
-        turn_w(3)
-
-        quantise_w(2)
-        quantise_w(3)
-
-        z_sb = keep.tile([P, D], F32)
-        nc.scalar.copy(
+        scalar_copy(
             out=z_sb[:].rearrange("n (q j) -> n q j", j=GROUPS),
             in_=z_ps[:].rearrange("n (j q) -> n q j", j=GROUPS),
         )
         nc.sync.dma_start(out=out_1, in_=z_sb[:])
 
-        logits_sb = keep.tile([P, OUT], F32)
-        for h in range(OUT_CHUNKS // CHUNKS_PER_BANK):
-            logits_ps = finished.tile([P, CHUNKS_PER_BANK, P], F32)
-            for c in range(CHUNKS_PER_BANK):
-                oc = h * CHUNKS_PER_BANK + c
-                nc.tensor.matmul_mx(
-                    out=logits_ps[:, c, :],
-                    lhsT=x_codes[:].bitcast(FP8X4),
-                    lhsT_scale=x_scales[:],
-                    rhs=w_codes[:, oc, 0, :].bitcast(FP8X4),
-                    rhs_scale=w_scales[:, oc, 0, :],
-                    start=True,
-                    stop=False,
-                )
-                nc.tensor.matmul_mx(
-                    out=logits_ps[:, c, :],
-                    lhsT=z_codes[:].bitcast(FP8X4),
-                    lhsT_scale=z_scales[:],
-                    rhs=w_codes[:, oc, 1, :].bitcast(FP8X4),
-                    rhs_scale=w_scales[:, oc, 1, :],
-                    start=False,
-                    stop=True,
-                )
-            cols = slice(h * CHUNKS_PER_BANK * P, (h + 1) * CHUNKS_PER_BANK * P)
-            nc.vector.tensor_tensor(
-                out=logits_sb[:, cols],
-                in0=logits_ps[:].rearrange("n c o -> n (c o)"),
-                in1=bias_sb[:, cols],
-                op=mybir.AluOpType.add,
-            )
-            nc.sync.dma_start(out=out_0[:, cols], in_=logits_sb[:, cols])
+        first_ps = sums.tile([P, 2, P], F32, tag="first")
+        for oc in range(2):
+            for g in range(W_PASSES):
+                multiply(first_ps[:, oc, :], oc, g)
+        third_ps = sums.tile([P, P], F32, tag="third")
+        for g in range(W_PASSES):
+            multiply(third_ps[:], 2, g)
+        last_ps = sums.tile([P, P], F32, tag="zt")
+        for g in range(W_PASSES):
+            multiply(last_ps[:], LAST, g)
+        finish(first_ps[:].rearrange("n c o -> n (c o)"), 0, 2)
+        finish(third_ps[:], 2, 3)
+        finish(last_ps[:], LAST, OUT_CHUNKS)

@@ -18,10 +18,9 @@ W_PASSES = 2
 GROUPS = D // P
 OUT_CHUNKS = OUT // P
 LAST = OUT_CHUNKS - 1
-WARM_COLS = 256
-WARM_PASSES = 8
+WARM_PASSES = 12
 
-VECTOR_Q = 88
+VECTOR_Q = 80
 
 FLOPS = 2 * P * K_PASS * D + 2 * P * (W_PASSES * K_PASS) * OUT
 
@@ -36,6 +35,8 @@ def tile_visualdeconfounder_pb_s_kernel(tc, att_prior, dic, x, cs_w, cs_b, out_0
 
         dic_raw = keep.tile([P, PACK, D], BF16)
         nc.sync.dma_start(out=dic_raw[:], in_=dic.rearrange("(p t) c -> p t c", t=PACK))
+        zeros = keep.tile([P, P, PACK], BF16, align_bytes=64)
+        nc.vector.memset(zeros[:].rearrange("p c t -> p (c t)").bitcast(U32), 0)
         bias_rows = keep.tile([P, OUT], BF16)
         nc.vector.memset(bias_rows[:].bitcast(U32), 0)
         nc.sync.dma_start(out=bias_rows[0:1, :], in_=cs_b.unsqueeze(0))
@@ -49,8 +50,6 @@ def tile_visualdeconfounder_pb_s_kernel(tc, att_prior, dic, x, cs_w, cs_b, out_0
 
         ident = keep.tile([P, P], F32)
         make_identity(nc, ident[:])
-        zeros = keep.tile([P, WARM_COLS, PACK], BF16, align_bytes=64)
-        nc.vector.memset(zeros[:].rearrange("p c t -> p (c t)").bitcast(U32), 0)
         ones = keep.tile([P, P], BF16)
         nc.vector.memset(ones[:], 1.0)
 
@@ -117,40 +116,39 @@ def tile_visualdeconfounder_pb_s_kernel(tc, att_prior, dic, x, cs_w, cs_b, out_0
             nc.vector.tensor_tensor(out=logits_sb[:, cols], in0=acc, in1=bias_sb[:, cols], op=mybir.AluOpType.add)
             nc.sync.dma_start(out=out_0[:, cols], in_=logits_sb[:, cols])
 
-        zero_codes = keep.tile([P, WARM_COLS], U32, align_bytes=64)
-        zero_scales = keep.tile([P, WARM_COLS], U8, align_bytes=64)
+        zero_codes = keep.tile([P, P], U32, align_bytes=64)
+        zero_scales = keep.tile([P, P], U8, align_bytes=64)
         quantise(zeros[:], zero_codes[:], zero_scales[:])
-        warm_ps = sums.tile([P, WARM_COLS], F32, tag="rows")
+        warm_ps = sums.tile([P, P], F32, tag="rows")
         for i in range(WARM_PASSES):
             nc.tensor.matmul_mx(
                 out=warm_ps[:],
-                lhsT=zero_codes[:, :P].bitcast(FP8X4),
-                lhsT_scale=zero_scales[:, :P],
+                lhsT=zero_codes[:].bitcast(FP8X4),
+                lhsT_scale=zero_scales[:],
                 rhs=zero_codes[:].bitcast(FP8X4),
                 rhs_scale=zero_scales[:],
                 start=True,
                 stop=True,
             )
 
+        bias_ps = sums.tile([P, OUT], BF16, tag="rows")
+        nc.tensor.matmul(out=bias_ps[:], lhsT=ones[:], rhs=bias_rows[:], start=True, stop=True)
         dic_read = dic_raw[:].rearrange("p t (q j) -> p q j t", j=GROUPS)
         dic_write = dic_grouped[:].rearrange("p (j q) t -> p q j t", j=GROUPS)
         vector_copy(out=dic_write[:, :VECTOR_Q], in_=dic_read[:, :VECTOR_Q])
         scalar_copy(out=dic_write[:, VECTOR_Q:], in_=dic_read[:, VECTOR_Q:])
+        vector_copy(out=bias_sb[:], in_=bias_ps[:])
         att_t = turn(att_sb[:])
         regroup(scalar_copy, att_t, att_grouped[:])
         x_t = turn(x_sb[:])
         regroup(scalar_copy, x_t, x_grouped[:])
-        bias_ps = sums.tile([P, OUT], BF16, tag="rows")
-        nc.tensor.matmul(out=bias_ps[:], lhsT=ones[:], rhs=bias_rows[:], start=True, stop=True)
-        for j in range(0, GROUPS, 2):
-            cols = slice(j * P, (j + 2) * P)
-            quantise(dic_grouped[:, cols, :], dic_codes[:, cols], dic_scales[:, cols])
+        quantise(dic_grouped[:], dic_codes[:], dic_scales[:])
         quantise(att_grouped[:, 0], att_codes[:], att_scales[:])
         quantise(x_grouped[:, 0], x_codes[:], x_scales[:])
-        vector_copy(out=bias_sb[:], in_=bias_ps[:])
 
-        for oc in range(2):
-            regroup(scalar_copy, turn(w_sb[:, oc, :]), w_grouped[:, oc])
+        regroup(scalar_copy, turn(w_sb[:, 0, :]), w_grouped[:, 0])
+        regroup(vector_copy, turn(w_sb[:, 1, :K_PASS]), w_grouped[:, 1, 0:1])
+        regroup(scalar_copy, turn(w_sb[:, 1, K_PASS:]), w_grouped[:, 1, 1:2])
         zt_ps = sums.tile([P, GROUPS, P], F32, tag="zt")
         for j in range(GROUPS):
             cols = slice(j * P, (j + 1) * P)
@@ -163,18 +161,6 @@ def tile_visualdeconfounder_pb_s_kernel(tc, att_prior, dic, x, cs_w, cs_b, out_0
                 start=True,
                 stop=True,
             )
-        scalar_copy(out=z_grouped[:], in_=zt_ps[:].rearrange("q j n -> q n j"))
-        quantise_w(0)
-        quantise_w(1)
-        regroup(vector_copy, turn(w_sb[:, 2, :K_PASS]), w_grouped[:, 2, 0:1])
-        regroup(scalar_copy, turn(w_sb[:, 2, K_PASS:]), w_grouped[:, 2, 1:2])
-        quantise(z_grouped[:], z_codes[:], z_scales[:])
-        regroup(scalar_copy, turn(w_sb[:, LAST, :K_PASS]), w_grouped[:, LAST, 0:1])
-        regroup(scalar_copy, turn(w_sb[:, LAST, K_PASS:]), w_grouped[:, LAST, 1:2])
-        quantise_w(2)
-        quantise_w(LAST, 0, 1)
-        quantise_w(LAST, 1, 2)
-
         z_ps = sums.tile([P, D], F32, tag="rows")
         nc.tensor.matmul_mx(
             out=z_ps[:],
@@ -185,6 +171,18 @@ def tile_visualdeconfounder_pb_s_kernel(tc, att_prior, dic, x, cs_w, cs_b, out_0
             start=True,
             stop=True,
         )
+        scalar_copy(out=z_grouped[:], in_=zt_ps[:].rearrange("q j n -> q n j"))
+        quantise_w(0)
+        quantise_w(1)
+        regroup(scalar_copy, turn(w_sb[:, 2, :K_PASS]), w_grouped[:, 2, 0:1])
+        regroup(vector_copy, turn(w_sb[:, 2, K_PASS:]), w_grouped[:, 2, 1:2])
+        quantise(z_grouped[:], z_codes[:], z_scales[:])
+        regroup(vector_copy, turn(w_sb[:, LAST, :K_PASS]), w_grouped[:, LAST, 0:1])
+        regroup(scalar_copy, turn(w_sb[:, LAST, K_PASS:]), w_grouped[:, LAST, 1:2])
+        quantise_w(2)
+        quantise_w(LAST, 0, 1)
+        quantise_w(LAST, 1, 2)
+
         scalar_copy(
             out=z_sb[:].rearrange("n (q j) -> n q j", j=GROUPS),
             in_=z_ps[:].rearrange("n (j q) -> n q j", j=GROUPS),

@@ -177,17 +177,17 @@ def tile_visualdeconfounder_pb_s_kernel(tc, att_prior, dic, x, cs_w, cs_b, out_0
         regroup(scalar_copy, turn(w_sb[:, 2, :K_PASS]), w_grouped[:, 2, 0:1])
         regroup(vector_copy, turn(w_sb[:, 2, K_PASS:]), w_grouped[:, 2, 1:2])
         quantise(z_grouped[:], z_codes[:], z_scales[:])
+        scalar_copy(
+            out=z_sb[:].rearrange("n (q j) -> n q j", j=GROUPS),
+            in_=z_ps[:].rearrange("n (j q) -> n q j", j=GROUPS),
+        )
+        nc.sync.dma_start(out=out_1, in_=z_sb[:])
         regroup(vector_copy, turn(w_sb[:, LAST, :K_PASS]), w_grouped[:, LAST, 0:1])
         regroup(scalar_copy, turn(w_sb[:, LAST, K_PASS:]), w_grouped[:, LAST, 1:2])
         quantise_w(2)
         quantise_w(LAST, 0, 1)
         quantise_w(LAST, 1, 2)
 
-        scalar_copy(
-            out=z_sb[:].rearrange("n (q j) -> n q j", j=GROUPS),
-            in_=z_ps[:].rearrange("n (j q) -> n q j", j=GROUPS),
-        )
-        nc.sync.dma_start(out=out_1, in_=z_sb[:])
 
         first_ps = sums.tile([P, 2, P], F32, tag="first")
         for oc in range(2):

from contextlib import ExitStack

import concourse.mybir as mybir
from concourse.masks import make_identity

BF16 = mybir.dt.bfloat16
F32 = mybir.dt.float32
U32 = mybir.dt.uint32
U8 = mybir.dt.uint8
FP8X4 = mybir.dt.float8_e4m3fn_x4

P = 128
PACK = 4
K_PASS = P * PACK
D = 512
OUT = 512
W_PASSES = 2
GROUPS = D // P
OUT_CHUNKS = OUT // P
LAST = OUT_CHUNKS - 1
WARM_PASSES = 12

VECTOR_Q = 80

FLOPS = 2 * P * K_PASS * D + 2 * P * (W_PASSES * K_PASS) * OUT


def tile_visualdeconfounder_pb_s_kernel(tc, att_prior, dic, x, cs_w, cs_b, out_0, out_1):
    nc = tc.nc
    with ExitStack() as ctx:
        keep = ctx.enter_context(tc.tile_pool(name="keep", bufs=1))
        turned = ctx.enter_context(tc.psum_pool(name="turned", bufs=4))
        sums = ctx.enter_context(tc.psum_pool(name="sums", bufs=1))
        ctx.enter_context(tc.manual_schedule())

        dic_raw = keep.tile([P, PACK, D], BF16)
        nc.sync.dma_start(out=dic_raw[:], in_=dic.rearrange("(p t) c -> p t c", t=PACK))
        zeros = keep.tile([P, P, PACK], BF16, align_bytes=64)
        nc.vector.memset(zeros[:].rearrange("p c t -> p (c t)").bitcast(U32), 0)
        bias_rows = keep.tile([P, OUT], BF16)
        nc.vector.memset(bias_rows[:].bitcast(U32), 0)
        nc.sync.dma_start(out=bias_rows[0:1, :], in_=cs_b.unsqueeze(0))
        att_sb = keep.tile([P, K_PASS], BF16)
        nc.sync.dma_start(out=att_sb[:], in_=att_prior)
        x_sb = keep.tile([P, K_PASS], BF16)
        nc.sync.dma_start(out=x_sb[:], in_=x)
        w_sb = keep.tile([P, OUT_CHUNKS, W_PASSES * K_PASS], BF16)
        for oc in range(OUT_CHUNKS):
            nc.sync.dma_start(out=w_sb[:, oc, :], in_=cs_w[oc * P : (oc + 1) * P, :])

        ident = keep.tile([P, P], F32)
        make_identity(nc, ident[:])
        ones = keep.tile([P, P], BF16)
        nc.vector.memset(ones[:], 1.0)

        def turn(rows_sb):
            words = rows_sb.bitcast(F32)
            tiles = words.shape[1] // P
            words_t = turned.tile([P, PACK, P], F32, tag="turned")
            for gu in range(tiles):
                first = 2 * P * (gu // 2) + gu % 2
                nc.tensor.transpose(words_t[:, gu, :], words[:, first : first + 2 * P - 1 : 2], ident[:])
            return words_t[:, :tiles, :]

        def regroup(engine_copy, words_t, grouped):
            engine_copy(out=grouped.bitcast(F32), in_=words_t.rearrange("p (g u) r -> p g r u", u=2))

        def quantise(grouped, codes, scales):
            nc.vector.quantize_mx(
                out=codes.bitcast(FP8X4), scales=scales, in_=grouped.rearrange("p c t -> p (c t)")
            )

        scalar_copy = nc.scalar.copy
        vector_copy = nc.vector.tensor_copy

        att_grouped = keep.tile([P, 1, P, PACK], BF16, align_bytes=64)
        att_codes = keep.tile([P, P], U32, align_bytes=64)
        att_scales = keep.tile([P, P], U8, align_bytes=64)
        x_grouped = keep.tile([P, 1, P, PACK], BF16, align_bytes=64)
        x_codes = keep.tile([P, P], U32, align_bytes=64)
        x_scales = keep.tile([P, P], U8, align_bytes=64)
        dic_grouped = keep.tile([P, D, PACK], BF16, align_bytes=64)
        dic_codes = keep.tile([P, D], U32, align_bytes=64)
        dic_scales = keep.tile([P, D], U8, align_bytes=64)
        w_grouped = keep.tile([P, OUT_CHUNKS, W_PASSES, P, PACK], BF16, align_bytes=64)
        w_codes = keep.tile([P, OUT_CHUNKS, W_PASSES, P], U32, align_bytes=64)
        w_scales = keep.tile([P, OUT_CHUNKS, W_PASSES, P], U8, align_bytes=64)
        z_grouped = keep.tile([P, P, PACK], BF16, align_bytes=64)
        z_codes = keep.tile([P, P], U32, align_bytes=64)
        z_scales = keep.tile([P, P], U8, align_bytes=64)
        bias_sb = keep.tile([P, OUT], BF16)
        z_sb = keep.tile([P, D], F32)
        logits_sb = keep.tile([P, OUT], F32)

        def quantise_w(oc, first=0, last=W_PASSES):
            quantise(
                w_grouped[:, oc, first:last].rearrange("p g o t -> p (g o) t"),
                w_codes[:, oc, first:last].rearrange("p g o -> p (g o)"),
                w_scales[:, oc, first:last].rearrange("p g o -> p (g o)"),
            )

        def multiply(acc, oc, g):
            codes, scales = ((x_codes, x_scales), (z_codes, z_scales))[g]
            nc.tensor.matmul_mx(
                out=acc,
                lhsT=codes[:].bitcast(FP8X4),
                lhsT_scale=scales[:],
                rhs=w_codes[:, oc, g, :].bitcast(FP8X4),
                rhs_scale=w_scales[:, oc, g, :],
                start=g == 0,
                stop=g == W_PASSES - 1,
            )

        def finish(acc, first, last):
            cols = slice(first * P, last * P)
            nc.vector.tensor_tensor(out=logits_sb[:, cols], in0=acc, in1=bias_sb[:, cols], op=mybir.AluOpType.add)
            nc.sync.dma_start(out=out_0[:, cols], in_=logits_sb[:, cols])

        zero_codes = keep.tile([P, P], U32, align_bytes=64)
        zero_scales = keep.tile([P, P], U8, align_bytes=64)
        quantise(zeros[:], zero_codes[:], zero_scales[:])
        warm_ps = sums.tile([P, P], F32, tag="rows")
        for i in range(WARM_PASSES):
            nc.tensor.matmul_mx(
                out=warm_ps[:],
                lhsT=zero_codes[:].bitcast(FP8X4),
                lhsT_scale=zero_scales[:],
                rhs=zero_codes[:].bitcast(FP8X4),
                rhs_scale=zero_scales[:],
                start=True,
                stop=True,
            )

        bias_ps = sums.tile([P, OUT], BF16, tag="rows")
        nc.tensor.matmul(out=bias_ps[:], lhsT=ones[:], rhs=bias_rows[:], start=True, stop=True)
        dic_read = dic_raw[:].rearrange("p t (q j) -> p q j t", j=GROUPS)
        dic_write = dic_grouped[:].rearrange("p (j q) t -> p q j t", j=GROUPS)
        vector_copy(out=dic_write[:, :VECTOR_Q], in_=dic_read[:, :VECTOR_Q])
        scalar_copy(out=dic_write[:, VECTOR_Q:], in_=dic_read[:, VECTOR_Q:])
        vector_copy(out=bias_sb[:], in_=bias_ps[:])
        att_t = turn(att_sb[:])
        regroup(scalar_copy, att_t, att_grouped[:])
        x_t = turn(x_sb[:])
        regroup(scalar_copy, x_t, x_grouped[:])
        quantise(dic_grouped[:], dic_codes[:], dic_scales[:])
        quantise(att_grouped[:, 0], att_codes[:], att_scales[:])
        quantise(x_grouped[:, 0], x_codes[:], x_scales[:])

        regroup(scalar_copy, turn(w_sb[:, 0, :]), w_grouped[:, 0])
        regroup(vector_copy, turn(w_sb[:, 1, :K_PASS]), w_grouped[:, 1, 0:1])
        regroup(scalar_copy, turn(w_sb[:, 1, K_PASS:]), w_grouped[:, 1, 1:2])
        zt_ps = sums.tile([P, GROUPS, P], F32, tag="zt")
        for j in range(GROUPS):
            cols = slice(j * P, (j + 1) * P)
            nc.tensor.matmul_mx(
                out=zt_ps[:, j, :],
                lhsT=dic_codes[:, cols].bitcast(FP8X4),
                lhsT_scale=dic_scales[:, cols],
                rhs=att_codes[:].bitcast(FP8X4),
                rhs_scale=att_scales[:],
                start=True,
                stop=True,
            )
        z_ps = sums.tile([P, D], F32, tag="rows")
        nc.tensor.matmul_mx(
            out=z_ps[:],
            lhsT=att_codes[:].bitcast(FP8X4),
            lhsT_scale=att_scales[:],
            rhs=dic_codes[:].bitcast(FP8X4),
            rhs_scale=dic_scales[:],
            start=True,
            stop=True,
        )
        scalar_copy(out=z_grouped[:], in_=zt_ps[:].rearrange("q j n -> q n j"))
        quantise_w(0)
        quantise_w(1)
        regroup(scalar_copy, turn(w_sb[:, 2, :K_PASS]), w_grouped[:, 2, 0:1])
        regroup(vector_copy, turn(w_sb[:, 2, K_PASS:]), w_grouped[:, 2, 1:2])
        quantise(z_grouped[:], z_codes[:], z_scales[:])
        scalar_copy(
            out=z_sb[:].rearrange("n (q j) -> n q j", j=GROUPS),
            in_=z_ps[:].rearrange("n (j q) -> n q j", j=GROUPS),
        )
        nc.sync.dma_start(out=out_1, in_=z_sb[:])
        regroup(vector_copy, turn(w_sb[:, LAST, :K_PASS]), w_grouped[:, LAST, 0:1])
        regroup(scalar_copy, turn(w_sb[:, LAST, K_PASS:]), w_grouped[:, LAST, 1:2])
        quantise_w(2)
        quantise_w(LAST, 0, 1)
        quantise_w(LAST, 1, 2)


        first_ps = sums.tile([P, 2, P], F32, tag="first")
        for oc in range(2):
            for g in range(W_PASSES):
                multiply(first_ps[:, oc, :], oc, g)
        third_ps = sums.tile([P, P], F32, tag="third")
        for g in range(W_PASSES):
            multiply(third_ps[:], 2, g)
        last_ps = sums.tile([P, P], F32, tag="zt")
        for g in range(W_PASSES):
            multiply(last_ps[:], LAST, g)
        finish(first_ps[:].rearrange("n c o -> n (c o)"), 0, 2)
        finish(third_ps[:], 2, 3)
        finish(last_ps[:], LAST, OUT_CHUNKS)
